import numpy as np
import ml_dtypes


def mxq(x, axis, fmt="e4m3"):
    dtype, down = {"e4m3": (ml_dtypes.float8_e4m3fn, 7), "e5m2": (ml_dtypes.float8_e5m2, 14)}[fmt]
    v = np.moveaxis(np.asarray(x, np.float32).astype(ml_dtypes.bfloat16).astype(np.float64), axis, -1)
    blocks = v.reshape(v.shape[:-1] + (-1, 32))
    amax = np.abs(blocks).max(-1, keepdims=True)
    byte = np.maximum(np.where(amax > 0, np.frexp(amax)[1] - 1 + 127, 0) - down, 1)
    scale = np.exp2(byte - 127.0)
    codes = (blocks / scale).astype(np.float32).astype(dtype).astype(np.float64)
    return np.moveaxis((codes * scale).reshape(v.shape), -1, axis)


WIDE = False


def mx_kscale(k):
    if not WIDE:
        return np.ones(k)
    levels = np.array([10, -10, 5, -5, 0])
    a = np.random.permutation(np.resize(levels, k // 512 * 4)).reshape(k // 512, 4)
    idx = np.arange(k)
    return np.exp2(a[idx // 512, idx % 128 // 32])


BF16 = ml_dtypes.bfloat16


def bf(x):
    return np.asarray(x, np.float32).astype(BF16)


def f64(x):
    return np.asarray(x).astype(np.float64)


E2M1 = np.array([0.0, 0.5, 1.0, 1.5, 2.0, 3.0, 4.0, 6.0, -0.0, -0.5, -1.0, -1.5, -2.0, -3.0, -4.0, -6.0])


def pack_weight(w, fmt):
    k, n = w.shape
    w = f64(bf(w)).reshape(k // 32, 32, n)
    amax = np.abs(w).max(1)
    if fmt == "e4m3":
        byte = np.frexp(amax)[1] - 1 + 127 - 7
    else:
        mant, ex = np.frexp(amax / 6.0)
        byte = np.where(mant > 0.5, ex, ex - 1) + 127
    byte = np.clip(np.where(amax > 0, byte, 1), 1, 254)
    scaled = (w * np.exp2(127.0 - byte)[:, None, :]).reshape(k, n).astype(np.float32)
    by_word = np.ascontiguousarray(scaled.reshape(k // 512, 128, 4, n).transpose(0, 1, 3, 2))
    if fmt == "e4m3":
        words = by_word.astype(ml_dtypes.float8_e4m3fn).view(np.uint8)
    else:
        c = by_word.astype(ml_dtypes.float4_e2m1fn).view(np.uint8) & 0xF
        words = c[..., 0::2] | (c[..., 1::2] << 4)
    return np.ascontiguousarray(words), np.ascontiguousarray(byte.astype(np.uint8).reshape(k // 512, 16, n))


def unpack_weight(words, scales, fmt):
    g, p, n, _ = words.shape
    if fmt == "e4m3":
        vals = np.ascontiguousarray(words).view(ml_dtypes.float8_e4m3fn).astype(np.float64)
    else:
        nib = np.empty((g, p, n, 4), np.uint8)
        nib[..., 0::2] = words & 0xF
        nib[..., 1::2] = words >> 4
        vals = E2M1[nib]
    vals = vals * np.repeat(np.exp2(scales.astype(np.float64) - 127.0), 8, axis=1)[..., None]
    return vals.transpose(0, 1, 3, 2).reshape(g * 512, n)


B, D, H = 2048, 512, 512
FMT = "e4m3"


def sigmoid(v):
    return 1.0 / (1.0 + np.exp(-v))


def setup_inputs():
    s, t = mx_kscale(D), mx_kscale(H)
    inp = {"input": bf(np.random.standard_normal((B, D)) * s),
           "h": bf(np.random.standard_normal((B, H)) * t),
           "c": bf(np.random.standard_normal((B, H)))}
    for gate in "ifgo":
        words, scales = pack_weight(np.random.standard_normal((D, H)) / np.sqrt(D) / s[:, None], FMT)
        inp["w_i" + gate + "_words"] = words
        inp["w_i" + gate + "_scales"] = scales
        words, scales = pack_weight(np.random.standard_normal((H, H)) / np.sqrt(H) / t[:, None], FMT)
        inp["w_h" + gate + "_words"] = words
        inp["w_h" + gate + "_scales"] = scales
        inp["b_i" + gate] = bf(np.random.standard_normal(H) * 0.3)
        inp["b_h" + gate] = bf(np.random.standard_normal(H) * 0.3)
    return inp


def reference(input, h, c,
              w_ii_words, w_ii_scales, w_hi_words, w_hi_scales, b_ii, b_hi,
              w_if_words, w_if_scales, w_hf_words, w_hf_scales, b_if, b_hf,
              w_ig_words, w_ig_scales, w_hg_words, w_hg_scales, b_ig, b_hg,
              w_io_words, w_io_scales, w_ho_words, w_ho_scales, b_io, b_ho):
    w_x = np.concatenate([unpack_weight(w_ii_words, w_ii_scales, FMT), unpack_weight(w_if_words, w_if_scales, FMT),
                          unpack_weight(w_ig_words, w_ig_scales, FMT), unpack_weight(w_io_words, w_io_scales, FMT)], axis=1)
    w_h = np.concatenate([unpack_weight(w_hi_words, w_hi_scales, FMT), unpack_weight(w_hf_words, w_hf_scales, FMT),
                          unpack_weight(w_hg_words, w_hg_scales, FMT), unpack_weight(w_ho_words, w_ho_scales, FMT)], axis=1)
    b = np.concatenate([f64(b_ii) + f64(b_hi), f64(b_if) + f64(b_hf), f64(b_ig) + f64(b_hg), f64(b_io) + f64(b_ho)])
    pre = (mxq(f64(input), 1, "e4m3") @ w_x) + (mxq(f64(h), 1, "e4m3") @ w_h) + b
    i, f, g, o = np.split(pre, 4, axis=1)
    i = sigmoid(i)
    f = sigmoid(f)
    g = sigmoid(g)
    o = sigmoid(o)
    c_prime = f * f64(c) + i * g
    h_prime = o * np.tanh(c_prime)
    return h_prime, c_prime

@@ -1,0 +1,254 @@
+from contextlib import ExitStack
+
+import concourse.mybir as mybir
+from concourse.masks import make_identity
+
+F32 = mybir.dt.float32
+BF16 = mybir.dt.bfloat16
+I32 = mybir.dt.int32
+U32 = mybir.dt.uint32
+U8 = mybir.dt.uint8
+FP8X4 = mybir.dt.float8_e4m3fn_x4
+SIGMOID = mybir.ActivationFunctionType.Sigmoid
+TANH = mybir.ActivationFunctionType.Tanh
+ADD = mybir.AluOpType.add
+MULT = mybir.AluOpType.mult
+
+P = 128
+BATCH = 2048
+K = 512
+HIDDEN = 512
+FLOPS = 2 * BATCH * (2 * K) * (4 * HIDDEN)
+
+TILES = BATCH // P
+CHUNKS = HIDDEN // P
+ROUND = 4
+STEP = 2
+STEPS = TILES // STEP
+LEAD_IN = 3
+LEAD_IG = 2
+GATE_SLOT = {"i": 0, "f": 1, "g": 2, "o": 3}
+SIDES = (0, 1)
+
+
+def tile_lstmcell_kernel(
+    tc, x, h, c,
+    w_ii_words, w_ii_scales, w_hi_words, w_hi_scales, b_ii, b_hi,
+    w_if_words, w_if_scales, w_hf_words, w_hf_scales, b_if, b_hf,
+    w_ig_words, w_ig_scales, w_hg_words, w_hg_scales, b_ig, b_hg,
+    w_io_words, w_io_scales, w_ho_words, w_ho_scales, b_io, b_ho,
+    h_out, c_out,
+):
+    nc = tc.nc
+    words_of = {"i": (w_ii_words, w_hi_words), "f": (w_if_words, w_hf_words),
+                "g": (w_ig_words, w_hg_words), "o": (w_io_words, w_ho_words)}
+    scales_of = {"i": (w_ii_scales, w_hi_scales), "f": (w_if_scales, w_hf_scales),
+                 "g": (w_ig_scales, w_hg_scales), "o": (w_io_scales, w_ho_scales)}
+    bias_of = {"i": (b_ii, b_hi), "f": (b_if, b_hf), "g": (b_ig, b_hg), "o": (b_io, b_ho)}
+
+    x_rows = x.rearrange("(p t) k -> p t k", t=TILES)
+    h_rows = h.rearrange("(p t) k -> p t k", t=TILES)
+    c_rows = c.rearrange("(p t) n -> p t n", t=TILES)
+    h_out_rows = h_out.rearrange("(p t) n -> p t n", t=TILES)
+    c_out_rows = c_out.rearrange("(p t) n -> p t n", t=TILES)
+
+    with ExitStack() as ctx:
+        keep = ctx.enter_context(tc.tile_pool(name="keep", bufs=1))
+        work = ctx.enter_context(tc.tile_pool(name="work", bufs=4))
+        psum_mx = ctx.enter_context(tc.psum_pool(name="psum_mx", bufs=4))
+        psum_in = ctx.enter_context(tc.psum_pool(name="psum_in", bufs=2))
+        psum_back = ctx.enter_context(tc.psum_pool(name="psum_back", bufs=2))
+        ctx.enter_context(tc.manual_schedule())
+
+        x_sb = keep.tile([P, TILES, K], BF16, name="x_sb")
+        h_sb = keep.tile([P, TILES, K], BF16, name="h_sb")
+        c_sb = keep.tile([P, TILES, HIDDEN], BF16, name="c_sb")
+        act_sb = (x_sb, h_sb)
+        act_rows = (x_rows, h_rows)
+        w_codes = keep.tile([P, 8, HIDDEN], U32, name="w_codes", align_bytes=64)
+        w_planes = keep.tile([P, 8, HIDDEN], U8, name="w_planes", align_bytes=64)
+        a_codes = keep.tile([P, 2, BATCH], U32, name="a_codes", align_bytes=64)
+        a_planes = keep.tile([P, 2, BATCH], U8, name="a_planes", align_bytes=64)
+        identity = keep.tile([P, P], F32, name="identity")
+        ones = keep.tile([P, P], BF16, name="ones")
+        bias_rows = keep.tile([P, 4, HIDDEN], BF16, name="bias_rows")
+        bias_fo = keep.tile([P, 2, HIDDEN], F32, name="bias_fo")
+        bias_ig = keep.tile([P, 2 * CHUNKS], F32, name="bias_ig")
+
+        nc.vector.memset(bias_rows[:], 0.0)
+        nc.vector.memset(w_planes[:].bitcast(I32), 0)
+        nc.vector.memset(ones[:], 1.0)
+        make_identity(nc, identity[:])
+
+        def load_bias(gate):
+            for side in SIDES:
+                nc.sync.dma_start(out=bias_rows[side:side + 1, GATE_SLOT[gate], :],
+                                  in_=bias_of[gate][side].rearrange("(o n) -> o n", o=1))
+
+        def load_rows(dst, src, step):
+            cut = slice(STEP * step, STEP * (step + 1))
+            nc.sync.dma_start(out=dst[:, cut, :], in_=src[:, cut, :])
+
+        def load_weight(gate):
+            for side in SIDES:
+                slot = 2 * GATE_SLOT[gate] + side
+                nc.sync.dma_start(out=w_codes[:, slot, :].bitcast(I32),
+                                  in_=words_of[gate][side][0].rearrange("p n t -> p (n t)").bitcast(I32))
+            for side in SIDES:
+                slot = 2 * GATE_SLOT[gate] + side
+                for quadrant in range(4):
+                    nc.sync.dma_start(
+                        out=w_planes[32 * quadrant:32 * quadrant + 4, slot, :].bitcast(I32),
+                        in_=scales_of[gate][side][0, 4 * quadrant:4 * quadrant + 4, :].bitcast(I32))
+
+        load_bias("i")
+        load_bias("g")
+        for step in range(2):
+            for side in SIDES:
+                load_rows(act_sb[side], act_rows[side], step)
+        load_weight("i")
+        load_weight("g")
+        for side in SIDES:
+            load_rows(act_sb[side], act_rows[side], 2)
+        load_bias("f")
+        load_bias("o")
+        load_weight("f")
+        load_weight("o")
+        for step in range(STEPS):
+            load_rows(c_sb, c_rows, step)
+            if step + LEAD_IN < STEPS:
+                for side in SIDES:
+                    load_rows(act_sb[side], act_rows[side], step + LEAD_IN)
+
+        def spread_bias_ig():
+            bank = psum_back.tile([P, HIDDEN], F32, name="back")
+            for n, gate in enumerate(("i", "g")):
+                for j in range(CHUNKS):
+                    col = 32 * (CHUNKS * n + j)
+                    nc.tensor.matmul(out=bank[:, col:col + 32],
+                                     lhsT=bias_rows[:, GATE_SLOT[gate], P * j:P * (j + 1)],
+                                     rhs=ones[:, 0:32], start=True, stop=True)
+            nc.vector.tensor_copy(
+                out=bias_ig[:],
+                in_=bank[:, 0:32 * 2 * CHUNKS].rearrange("p (n w) -> p n w", w=32)[:, :, 0])
+
+        def spread_bias_fo():
+            for n, gate in enumerate(("f", "o")):
+                bank = psum_back.tile([P, HIDDEN], F32, name="back")
+                nc.tensor.matmul(out=bank[:], lhsT=ones[:], rhs=bias_rows[:, GATE_SLOT[gate], :],
+                                 start=True, stop=True)
+                nc.vector.tensor_copy(out=bias_fo[:, n, :], in_=bank[:])
+
+        def transpose_in(step, side):
+            bank = psum_in.tile([P, 2, STEP * P], F32, name="turned")
+            for i in range(STEP):
+                row_words = act_sb[side][:, STEP * step + i, :].bitcast(F32)
+                for u in range(2):
+                    nc.tensor.transpose(bank[:, u, P * i:P * (i + 1)], row_words[:, u:K // 2:2], identity[:])
+            return bank
+
+        def regroup(side, bank):
+            grouped = work.tile([P, 4 * STEP * P], BF16, name="grouped%d" % side, bufs=2, align_bytes=64)
+            out = grouped[:].bitcast(F32).rearrange("p (b u) -> p b u", u=2)
+            in_ = bank[:].rearrange("p u b -> p b u")
+            if side == 0:
+                nc.scalar.copy(out=out, in_=in_)
+            else:
+                nc.vector.tensor_copy(out=out, in_=in_)
+            return grouped
+
+        def quantise(step, side, grouped):
+            cols = slice(STEP * P * step, STEP * P * (step + 1))
+            nc.vector.quantize_mx(out=a_codes[:, side, cols].bitcast(FP8X4),
+                                  scales=a_planes[:, side, cols], in_=grouped[:])
+
+        def gate_by_rows(gate, t):
+            acc = psum_mx.tile([P, HIDDEN], F32, name="acc")
+            rows = slice(P * t, P * (t + 1))
+            for side in SIDES:
+                slot = 2 * GATE_SLOT[gate] + side
+                nc.tensor.matmul_mx(out=acc[:],
+                                    lhsT=a_codes[:, side, rows].bitcast(FP8X4), lhsT_scale=a_planes[:, side, rows],
+                                    rhs=w_codes[:, slot, :].bitcast(FP8X4), rhs_scale=w_planes[:, slot, :],
+                                    start=(side == 0), stop=(side == 1))
+            return acc
+
+        def gate_by_units(gate, round_, j):
+            acc = psum_mx.tile([P, ROUND * P], F32, name="acc")
+            units = slice(P * j, P * (j + 1))
+            rows = slice(ROUND * P * round_, ROUND * P * (round_ + 1))
+            for side in SIDES:
+                slot = 2 * GATE_SLOT[gate] + side
+                nc.tensor.matmul_mx(out=acc[:],
+                                    lhsT=w_codes[:, slot, units].bitcast(FP8X4), lhsT_scale=w_planes[:, slot, units],
+                                    rhs=a_codes[:, side, rows].bitcast(FP8X4), rhs_scale=a_planes[:, side, rows],
+                                    start=(side == 0), stop=(side == 1))
+            return acc
+
+        ig_of = {}
+        forget_of = {}
+        out_gate_of = {}
+        tanh_of = {}
+
+        def tiles_of(step):
+            return range(STEP * step, STEP * (step + 1)) if 0 <= step < STEPS else ()
+
+        for step in range(-LEAD_IN, STEPS + 1):
+            ahead = step + LEAD_IN
+            back_of = {}
+            for t in tiles_of(step - 1):
+                back = psum_back.tile([P, HIDDEN], F32, name="back")
+                for j in range(CHUNKS):
+                    cols = slice(P * (t % ROUND), P * (t % ROUND + 1))
+                    nc.tensor.transpose(back[:, P * j:P * (j + 1)], ig_of[(t // ROUND, j)][:, cols], identity[:])
+                back_of[t] = back
+            turned = [transpose_in(ahead, side) for side in SIDES] if ahead < STEPS else []
+            if step == -LEAD_IG:
+                spread_bias_ig()
+            if step == -1:
+                spread_bias_fo()
+            if turned:
+                grouped_x = regroup(0, turned[0])
+            for t in tiles_of(step - 1):
+                c_new = work.tile([P, HIDDEN], F32, name="c_new", bufs=6)
+                nc.vector.tensor_tensor(out=c_new[:], in0=back_of[t][:], in1=forget_of[t][:], op=ADD)
+                nc.sync.dma_start(out=c_out_rows[:, t, :], in_=c_new[:])
+                tanh_c = work.tile([P, HIDDEN], F32, name="tanh_c")
+                nc.scalar.activation(out=tanh_c[:], in_=c_new[:], func=TANH)
+                tanh_of[t] = tanh_c
+            if turned:
+                grouped_h = regroup(1, turned[1])
+                quantise(ahead, 0, grouped_x)
+                quantise(ahead, 1, grouped_h)
+            for t in tiles_of(step - 1):
+                h_new = work.tile([P, HIDDEN], F32, name="h_new", bufs=6)
+                nc.gpsimd.tensor_tensor(out=h_new[:], in0=out_gate_of[t][:], in1=tanh_of[t][:], op=MULT)
+                nc.sync.dma_start(out=h_out_rows[:, t, :], in_=h_new[:])
+            sig_f_of = {}
+            for t in tiles_of(step):
+                for n, gate in enumerate(("f", "o")):
+                    acc = gate_by_rows(gate, t)
+                    pre = work.tile([P, HIDDEN], F32, name="pre")
+                    nc.vector.tensor_tensor(out=pre[:], in0=acc[:], in1=bias_fo[:, n, :], op=ADD)
+                    sig = work.tile([P, HIDDEN], F32, name="sig_" + gate, bufs=6)
+                    nc.scalar.activation(out=sig[:], in_=pre[:], func=SIGMOID)
+                    if gate == "f":
+                        sig_f_of[t] = sig
+                    else:
+                        out_gate_of[t] = sig
+            for m in tiles_of(step + LEAD_IG):
+                round_, j = m // CHUNKS, m % CHUNKS
+                sig_pair = []
+                for n, gate in enumerate(("i", "g")):
+                    acc = gate_by_units(gate, round_, j)
+                    sig = work.tile([P, ROUND * P], F32, name="sig_" + gate)
+                    col = CHUNKS * n + j
+                    nc.scalar.activation(out=sig[:], in_=acc[:], func=SIGMOID, bias=bias_ig[:, col:col + 1], scale=1.0)
+                    sig_pair.append(sig)
+                ig = work.tile([P, ROUND * P], F32, name="ig", bufs=2 * CHUNKS)
+                nc.gpsimd.tensor_tensor(out=ig[:], in0=sig_pair[0][:], in1=sig_pair[1][:], op=MULT)
+                ig_of[(round_, j)] = ig
+            for t in tiles_of(step):
+                forget = work.tile([P, HIDDEN], F32, name="forget")
+                nc.vector.tensor_tensor(out=forget[:], in0=sig_f_of[t][:], in1=c_sb[:, t, :], op=MULT)
+                forget_of[t] = forget

@@ -82,14 +82,14 @@ def tile_lstmcell_kernel(
 
         def load_bias(gate):
             for side in SIDES:
-                nc.sync.dma_start(out=bias_rows[side:side + 1, GATE_SLOT[gate], :],
-                                  in_=bias_of[gate][side].rearrange("(o n) -> o n", o=1))
+                nc.gpsimd.dma_start(out=bias_rows[side:side + 1, GATE_SLOT[gate], :],
+                                    in_=bias_of[gate][side].rearrange("(o n) -> o n", o=1))
 
         def load_rows(dst, src, step):
             cut = slice(STEP * step, STEP * (step + 1))
             nc.sync.dma_start(out=dst[:, cut, :], in_=src[:, cut, :])
 
-        def load_weight(gate):
+        def load_weight(gate, plane_queue, plane_view):
             for side in SIDES:
                 slot = 2 * GATE_SLOT[gate] + side
                 nc.sync.dma_start(out=w_codes[:, slot, :].bitcast(I32),
@@ -97,28 +97,27 @@ def tile_lstmcell_kernel(
             for side in SIDES:
                 slot = 2 * GATE_SLOT[gate] + side
                 for quadrant in range(4):
-                    nc.sync.dma_start(
-                        out=w_planes[32 * quadrant:32 * quadrant + 4, slot, :].bitcast(I32),
-                        in_=scales_of[gate][side][0, 4 * quadrant:4 * quadrant + 4, :].bitcast(I32))
+                    plane_queue.dma_start(
+                        out=w_planes[32 * quadrant:32 * quadrant + 4, slot, :].bitcast(plane_view),
+                        in_=scales_of[gate][side][0, 4 * quadrant:4 * quadrant + 4, :].bitcast(plane_view))
 
-        load_bias("i")
-        load_bias("g")
+        for gate in ("i", "g", "f", "o"):
+            load_bias(gate)
         for step in range(2):
             for side in SIDES:
                 load_rows(act_sb[side], act_rows[side], step)
-        load_weight("i")
-        load_weight("g")
-        for side in SIDES:
-            load_rows(act_sb[side], act_rows[side], 2)
-        load_bias("f")
-        load_bias("o")
-        load_weight("f")
-        load_weight("o")
+        load_weight("i", nc.sync, I32)
+        load_weight("g", nc.sync, I32)
+        for step in range(2, 4):
+            for side in SIDES:
+                load_rows(act_sb[side], act_rows[side], step)
+        load_weight("f", nc.sync, I32)
+        load_weight("o", nc.gpsimd, F32)
         for step in range(STEPS):
             load_rows(c_sb, c_rows, step)
-            if step + LEAD_IN < STEPS:
+            if step + 4 < STEPS:
                 for side in SIDES:
-                    load_rows(act_sb[side], act_rows[side], step + LEAD_IN)
+                    load_rows(act_sb[side], act_rows[side], step + 4)
 
         def spread_bias_ig():
             bank = psum_back.tile([P, HIDDEN], F32, name="back")

@@ -82,37 +82,37 @@ def tile_lstmcell_kernel(
 
         def load_bias(gate):
             for side in SIDES:
-                nc.gpsimd.dma_start(out=bias_rows[side:side + 1, GATE_SLOT[gate], :],
-                                    in_=bias_of[gate][side].rearrange("(o n) -> o n", o=1))
+                nc.sync.dma_start(out=bias_rows[side:side + 1, GATE_SLOT[gate], :],
+                                  in_=bias_of[gate][side].rearrange("(o n) -> o n", o=1))
 
         def load_rows(dst, src, step):
             cut = slice(STEP * step, STEP * (step + 1))
             nc.sync.dma_start(out=dst[:, cut, :], in_=src[:, cut, :])
 
-        def load_weight(gate, plane_queue, plane_view):
+        def load_words(gate):
             for side in SIDES:
                 slot = 2 * GATE_SLOT[gate] + side
                 nc.sync.dma_start(out=w_codes[:, slot, :].bitcast(I32),
                                   in_=words_of[gate][side][0].rearrange("p n t -> p (n t)").bitcast(I32))
-            for side in SIDES:
+
+        def load_planes(gate):
+            for side, queue, view in ((0, nc.sync, I32), (1, nc.gpsimd, F32)):
                 slot = 2 * GATE_SLOT[gate] + side
                 for quadrant in range(4):
-                    plane_queue.dma_start(
-                        out=w_planes[32 * quadrant:32 * quadrant + 4, slot, :].bitcast(plane_view),
-                        in_=scales_of[gate][side][0, 4 * quadrant:4 * quadrant + 4, :].bitcast(plane_view))
+                    queue.dma_start(
+                        out=w_planes[32 * quadrant:32 * quadrant + 4, slot, :].bitcast(view),
+                        in_=scales_of[gate][side][0, 4 * quadrant:4 * quadrant + 4, :].bitcast(view))
 
-        for gate in ("i", "g", "f", "o"):
-            load_bias(gate)
-        for step in range(2):
-            for side in SIDES:
-                load_rows(act_sb[side], act_rows[side], step)
-        load_weight("i", nc.sync, I32)
-        load_weight("g", nc.sync, I32)
-        for step in range(2, 4):
-            for side in SIDES:
-                load_rows(act_sb[side], act_rows[side], step)
-        load_weight("f", nc.sync, I32)
-        load_weight("o", nc.gpsimd, F32)
+        for first, gate_pair in ((0, ("i", "g")), (2, ("f", "o"))):
+            for gate in gate_pair:
+                load_bias(gate)
+            for step in (first, first + 1):
+                for side in SIDES:
+                    load_rows(act_sb[side], act_rows[side], step)
+            for gate in gate_pair:
+                load_words(gate)
+            for gate in gate_pair:
+                load_planes(gate)
         for step in range(STEPS):
             load_rows(c_sb, c_rows, step)
             if step + 4 < STEPS:
@@ -221,7 +221,8 @@ def tile_lstmcell_kernel(
                 quantise(ahead, 1, grouped_h)
             for t in tiles_of(step - 1):
                 h_new = work.tile([P, HIDDEN], F32, name="h_new", bufs=6)
-                nc.gpsimd.tensor_tensor(out=h_new[:], in0=out_gate_of[t][:], in1=tanh_of[t][:], op=MULT)
+                multiplier = nc.vector if step == STEPS else nc.gpsimd
+                multiplier.tensor_tensor(out=h_new[:], in0=out_gate_of[t][:], in1=tanh_of[t][:], op=MULT)
                 nc.sync.dma_start(out=h_out_rows[:, t, :], in_=h_new[:])
             sig_f_of = {}
             for t in tiles_of(step):
@@ -235,19 +236,21 @@ def tile_lstmcell_kernel(
                         sig_f_of[t] = sig
                     else:
                         out_gate_of[t] = sig
-            for m in tiles_of(step + LEAD_IG):
-                round_, j = m // CHUNKS, m % CHUNKS
-                sig_pair = []
-                for n, gate in enumerate(("i", "g")):
+            sig_of = {}
+            for n, gate in enumerate(("i", "g")):
+                for m in tiles_of(step + LEAD_IG):
+                    round_, j = m // CHUNKS, m % CHUNKS
                     acc = gate_by_units(gate, round_, j)
                     sig = work.tile([P, ROUND * P], F32, name="sig_" + gate)
                     col = CHUNKS * n + j
                     nc.scalar.activation(out=sig[:], in_=acc[:], func=SIGMOID, bias=bias_ig[:, col:col + 1], scale=1.0)
-                    sig_pair.append(sig)
+                    sig_of[(gate, m)] = sig
+            for m in tiles_of(step + LEAD_IG):
                 ig = work.tile([P, ROUND * P], F32, name="ig", bufs=2 * CHUNKS)
-                nc.gpsimd.tensor_tensor(out=ig[:], in0=sig_pair[0][:], in1=sig_pair[1][:], op=MULT)
-                ig_of[(round_, j)] = ig
+                nc.gpsimd.tensor_tensor(out=ig[:], in0=sig_of[("i", m)][:], in1=sig_of[("g", m)][:], op=MULT)
+                ig_of[(m // CHUNKS, m % CHUNKS)] = ig
             for t in tiles_of(step):
                 forget = work.tile([P, HIDDEN], F32, name="forget")
-                nc.vector.tensor_tensor(out=forget[:], in0=sig_f_of[t][:], in1=c_sb[:, t, :], op=MULT)
+                multiplier = nc.vector if tiles_of(step + LEAD_IG) else nc.gpsimd
+                multiplier.tensor_tensor(out=forget[:], in0=sig_f_of[t][:], in1=c_sb[:, t, :], op=MULT)
                 forget_of[t] = forget

@@ -75,8 +75,8 @@ def tile_lstmcell_kernel(
         bias_fo = keep.tile([P, 2, HIDDEN], F32, name="bias_fo")
         bias_ig = keep.tile([P, 2 * CHUNKS], F32, name="bias_ig")
 
-        nc.vector.memset(bias_rows[:], 0.0)
         nc.vector.memset(w_planes[:].bitcast(I32), 0)
+        nc.vector.memset(bias_rows[:].bitcast(F32), 0.0)
         nc.vector.memset(ones[:], 1.0)
         make_identity(nc, identity[:])
 
@@ -95,29 +95,37 @@ def tile_lstmcell_kernel(
                 nc.sync.dma_start(out=w_codes[:, slot, :].bitcast(I32),
                                   in_=words_of[gate][side][0].rearrange("p n t -> p (n t)").bitcast(I32))
 
-        def load_planes(gate):
-            for side, queue, view in ((0, nc.sync, I32), (1, nc.gpsimd, F32)):
+        def load_planes(gate, queue, view):
+            for side in SIDES:
                 slot = 2 * GATE_SLOT[gate] + side
                 for quadrant in range(4):
                     queue.dma_start(
                         out=w_planes[32 * quadrant:32 * quadrant + 4, slot, :].bitcast(view),
                         in_=scales_of[gate][side][0, 4 * quadrant:4 * quadrant + 4, :].bitcast(view))
 
-        for first, gate_pair in ((0, ("i", "g")), (2, ("f", "o"))):
-            for gate in gate_pair:
-                load_bias(gate)
-            for step in (first, first + 1):
-                for side in SIDES:
-                    load_rows(act_sb[side], act_rows[side], step)
-            for gate in gate_pair:
-                load_words(gate)
-            for gate in gate_pair:
-                load_planes(gate)
+        def load_acts(step):
+            for side in SIDES:
+                load_rows(act_sb[side], act_rows[side], step)
+
+        load_planes("o", nc.gpsimd, F32)
+        load_acts(0)
+        load_acts(1)
+        for gate in ("i", "g"):
+            load_bias(gate)
+        for gate in ("i", "g"):
+            load_planes(gate, nc.sync, I32)
+            load_words(gate)
+        load_acts(2)
+        load_acts(3)
+        for gate in ("f", "o"):
+            load_bias(gate)
+        load_planes("f", nc.sync, I32)
+        load_words("f")
+        load_words("o")
         for step in range(STEPS):
             load_rows(c_sb, c_rows, step)
             if step + 4 < STEPS:
-                for side in SIDES:
-                    load_rows(act_sb[side], act_rows[side], step + 4)
+                load_acts(step + 4)
 
         def spread_bias_ig():
             bank = psum_back.tile([P, HIDDEN], F32, name="back")

@@ -259,6 +259,5 @@ def tile_lstmcell_kernel(
                 ig_of[(m // CHUNKS, m % CHUNKS)] = ig
             for t in tiles_of(step):
                 forget = work.tile([P, HIDDEN], F32, name="forget")
-                multiplier = nc.vector if tiles_of(step + LEAD_IG) else nc.gpsimd
-                multiplier.tensor_tensor(out=forget[:], in0=sig_f_of[t][:], in1=c_sb[:, t, :], op=MULT)
+                nc.vector.tensor_tensor(out=forget[:], in0=sig_f_of[t][:], in1=c_sb[:, t, :], op=MULT)
                 forget_of[t] = forget

@@ -25,7 +25,7 @@ CHUNKS = HIDDEN // P
 ROUND = 4
 STEP = 2
 STEPS = TILES // STEP
-LEAD_IN = 3
+LEAD_IN = 4
 LEAD_IG = 2
 GATE_SLOT = {"i": 0, "f": 1, "g": 2, "o": 3}
 SIDES = (0, 1)
@@ -123,9 +123,9 @@ def tile_lstmcell_kernel(
         load_words("f")
         load_words("o")
         for step in range(STEPS):
-            load_rows(c_sb, c_rows, step)
             if step + 4 < STEPS:
                 load_acts(step + 4)
+            load_rows(c_sb, c_rows, step)
 
         def spread_bias_ig():
             bank = psum_back.tile([P, HIDDEN], F32, name="back")
@@ -200,6 +200,12 @@ def tile_lstmcell_kernel(
         def tiles_of(step):
             return range(STEP * step, STEP * (step + 1)) if 0 <= step < STEPS else ()
 
+        def turn_ahead(step):
+            turned = [transpose_in(step, side) for side in SIDES]
+            grouped = [regroup(side, turned[side]) for side in SIDES]
+            for side in SIDES:
+                quantise(step, side, grouped[side])
+
         for step in range(-LEAD_IN, STEPS + 1):
             ahead = step + LEAD_IN
             back_of = {}
@@ -209,13 +215,10 @@ def tile_lstmcell_kernel(
                     cols = slice(P * (t % ROUND), P * (t % ROUND + 1))
                     nc.tensor.transpose(back[:, P * j:P * (j + 1)], ig_of[(t // ROUND, j)][:, cols], identity[:])
                 back_of[t] = back
-            turned = [transpose_in(ahead, side) for side in SIDES] if ahead < STEPS else []
             if step == -LEAD_IG:
                 spread_bias_ig()
             if step == -1:
                 spread_bias_fo()
-            if turned:
-                grouped_x = regroup(0, turned[0])
             for t in tiles_of(step - 1):
                 c_new = work.tile([P, HIDDEN], F32, name="c_new", bufs=6)
                 nc.vector.tensor_tensor(out=c_new[:], in0=back_of[t][:], in1=forget_of[t][:], op=ADD)
@@ -223,10 +226,6 @@ def tile_lstmcell_kernel(
                 tanh_c = work.tile([P, HIDDEN], F32, name="tanh_c")
                 nc.scalar.activation(out=tanh_c[:], in_=c_new[:], func=TANH)
                 tanh_of[t] = tanh_c
-            if turned:
-                grouped_h = regroup(1, turned[1])
-                quantise(ahead, 0, grouped_x)
-                quantise(ahead, 1, grouped_h)
             for t in tiles_of(step - 1):
                 h_new = work.tile([P, HIDDEN], F32, name="h_new", bufs=6)
                 multiplier = nc.vector if step == STEPS else nc.gpsimd
@@ -244,6 +243,8 @@ def tile_lstmcell_kernel(
                         sig_f_of[t] = sig
                     else:
                         out_gate_of[t] = sig
+            if 0 <= step and ahead < STEPS:
+                turn_ahead(ahead)
             sig_of = {}
             for n, gate in enumerate(("i", "g")):
                 for m in tiles_of(step + LEAD_IG):
@@ -257,6 +258,8 @@ def tile_lstmcell_kernel(
                 ig = work.tile([P, ROUND * P], F32, name="ig", bufs=2 * CHUNKS)
                 nc.gpsimd.tensor_tensor(out=ig[:], in0=sig_of[("i", m)][:], in1=sig_of[("g", m)][:], op=MULT)
                 ig_of[(m // CHUNKS, m % CHUNKS)] = ig
+            if step < 0:
+                turn_ahead(ahead)
             for t in tiles_of(step):
                 forget = work.tile([P, HIDDEN], F32, name="forget")
                 nc.vector.tensor_tensor(out=forget[:], in0=sig_f_of[t][:], in1=c_sb[:, t, :], op=MULT)

@@ -202,9 +202,16 @@ def tile_lstmcell_kernel(
 
         def turn_ahead(step):
             turned = [transpose_in(step, side) for side in SIDES]
-            grouped = [regroup(side, turned[side]) for side in SIDES]
+            return [regroup(side, turned[side]) for side in SIDES]
+
+        def quantise_both(step, grouped):
             for side in SIDES:
                 quantise(step, side, grouped[side])
+
+        def h_prime(engine, t):
+            h_new = work.tile([P, HIDDEN], F32, name="h_new", bufs=6)
+            engine.tensor_tensor(out=h_new[:], in0=out_gate_of[t][:], in1=tanh_of[t][:], op=MULT)
+            nc.sync.dma_start(out=h_out_rows[:, t, :], in_=h_new[:])
 
         for step in range(-LEAD_IN, STEPS + 1):
             ahead = step + LEAD_IN
@@ -226,14 +233,13 @@ def tile_lstmcell_kernel(
                 tanh_c = work.tile([P, HIDDEN], F32, name="tanh_c")
                 nc.scalar.activation(out=tanh_c[:], in_=c_new[:], func=TANH)
                 tanh_of[t] = tanh_c
+            on_vector = [t for t in tiles_of(step - 1) if t % ROUND == 0 or step == STEPS]
             for t in tiles_of(step - 1):
-                h_new = work.tile([P, HIDDEN], F32, name="h_new", bufs=6)
-                multiplier = nc.vector if step == STEPS else nc.gpsimd
-                multiplier.tensor_tensor(out=h_new[:], in0=out_gate_of[t][:], in1=tanh_of[t][:], op=MULT)
-                nc.sync.dma_start(out=h_out_rows[:, t, :], in_=h_new[:])
+                if t not in on_vector:
+                    h_prime(nc.gpsimd, t)
             sig_f_of = {}
-            for t in tiles_of(step):
-                for n, gate in enumerate(("f", "o")):
+            for n, gate in enumerate(("f", "o")):
+                for t in tiles_of(step):
                     acc = gate_by_rows(gate, t)
                     pre = work.tile([P, HIDDEN], F32, name="pre")
                     nc.vector.tensor_tensor(out=pre[:], in0=acc[:], in1=bias_fo[:, n, :], op=ADD)
@@ -243,8 +249,9 @@ def tile_lstmcell_kernel(
                         sig_f_of[t] = sig
                     else:
                         out_gate_of[t] = sig
+            grouped = None
             if 0 <= step and ahead < STEPS:
-                turn_ahead(ahead)
+                grouped = turn_ahead(ahead)
             sig_of = {}
             for n, gate in enumerate(("i", "g")):
                 for m in tiles_of(step + LEAD_IG):
@@ -259,8 +266,12 @@ def tile_lstmcell_kernel(
                 nc.gpsimd.tensor_tensor(out=ig[:], in0=sig_of[("i", m)][:], in1=sig_of[("g", m)][:], op=MULT)
                 ig_of[(m // CHUNKS, m % CHUNKS)] = ig
             if step < 0:
-                turn_ahead(ahead)
+                grouped = turn_ahead(ahead)
             for t in tiles_of(step):
                 forget = work.tile([P, HIDDEN], F32, name="forget")
                 nc.vector.tensor_tensor(out=forget[:], in0=sig_f_of[t][:], in1=c_sb[:, t, :], op=MULT)
                 forget_of[t] = forget
+            if grouped:
+                quantise_both(ahead, grouped)
+            for t in on_vector:
+                h_prime(nc.vector, t)

@@ -224,8 +224,6 @@ def tile_lstmcell_kernel(
                 back_of[t] = back
             if step == -LEAD_IG:
                 spread_bias_ig()
-            if step == -1:
-                spread_bias_fo()
             for t in tiles_of(step - 1):
                 c_new = work.tile([P, HIDDEN], F32, name="c_new", bufs=6)
                 nc.vector.tensor_tensor(out=c_new[:], in0=back_of[t][:], in1=forget_of[t][:], op=ADD)
@@ -233,9 +231,11 @@ def tile_lstmcell_kernel(
                 tanh_c = work.tile([P, HIDDEN], F32, name="tanh_c")
                 nc.scalar.activation(out=tanh_c[:], in_=c_new[:], func=TANH)
                 tanh_of[t] = tanh_c
-            on_vector = [t for t in tiles_of(step - 1) if t % ROUND == 0 or step == STEPS]
+            on_vector = [t for t in tiles_of(step - 1) if (t % ROUND == 0 and t < TILES - ROUND) or step == STEPS]
+            if step == STEPS:
+                on_vector.insert(0, TILES - ROUND)
             for t in tiles_of(step - 1):
-                if t not in on_vector:
+                if t not in on_vector and t != TILES - ROUND:
                     h_prime(nc.gpsimd, t)
             sig_f_of = {}
             for n, gate in enumerate(("f", "o")):
@@ -265,6 +265,8 @@ def tile_lstmcell_kernel(
                 ig = work.tile([P, ROUND * P], F32, name="ig", bufs=2 * CHUNKS)
                 nc.gpsimd.tensor_tensor(out=ig[:], in0=sig_of[("i", m)][:], in1=sig_of[("g", m)][:], op=MULT)
                 ig_of[(m // CHUNKS, m % CHUNKS)] = ig
+            if step == -1:
+                spread_bias_fo()
             if step < 0:
                 grouped = turn_ahead(ahead)
             for t in tiles_of(step):

@@ -231,7 +231,8 @@ def tile_lstmcell_kernel(
                 tanh_c = work.tile([P, HIDDEN], F32, name="tanh_c")
                 nc.scalar.activation(out=tanh_c[:], in_=c_new[:], func=TANH)
                 tanh_of[t] = tanh_c
-            on_vector = [t for t in tiles_of(step - 1) if (t % ROUND == 0 and t < TILES - ROUND) or step == STEPS]
+            on_vector = [t for t in tiles_of(step - 1)
+                         if ((t % ROUND == 0 or t % (2 * ROUND) == 2) and t != TILES - ROUND) or step == STEPS]
             if step == STEPS:
                 on_vector.insert(0, TILES - ROUND)
             for t in tiles_of(step - 1):

@@ -27,7 +27,7 @@ STEP = 2
 STEPS = TILES // STEP
 LEAD_IN = 4
 LEAD_IG = 2
-GATE_SLOT = {"i": 0, "f": 1, "g": 2, "o": 3}
+GATE_SLOT = {"i": 0, "g": 1, "f": 2, "o": 3}
 SIDES = (0, 1)
 
 
@@ -75,9 +75,11 @@ def tile_lstmcell_kernel(
         bias_fo = keep.tile([P, 2, HIDDEN], F32, name="bias_fo")
         bias_ig = keep.tile([P, 2 * CHUNKS], F32, name="bias_ig")
 
-        nc.vector.memset(w_planes[:].bitcast(I32), 0)
-        nc.vector.memset(bias_rows[:].bitcast(F32), 0.0)
         nc.vector.memset(ones[:], 1.0)
+        nc.vector.memset(bias_rows[:].bitcast(F32), 0.0)
+        nc.vector.memset(w_planes[:].bitcast(I32), 0)
+        warm = keep.tile([P, 1], F32, name="warm")
+        nc.scalar.activation(out=warm[:], in_=ones[:, 0:1], func=SIGMOID)
         make_identity(nc, identity[:])
 
         def load_bias(gate):
@@ -107,37 +109,53 @@ def tile_lstmcell_kernel(
             for side in SIDES:
                 load_rows(act_sb[side], act_rows[side], step)
 
-        load_planes("o", nc.gpsimd, F32)
+
+        stage = keep.tile([16, 8, HIDDEN], U8, name="stage")
+        def load_bias2(gate):
+            for side in SIDES:
+                nc.gpsimd.dma_start(out=bias_rows[side:side + 1, GATE_SLOT[gate], :],
+                                  in_=bias_of[gate][side].rearrange("(o n) -> o n", o=1))
+        def load_stage(gate):
+            for side in SIDES:
+                slot = 2 * GATE_SLOT[gate] + side
+                nc.sync.dma_start(out=stage[:, slot, :].bitcast(I32), in_=scales_of[gate][side][0].bitcast(I32))
+        def spread(s, n):
+            for q in range(4):
+                nc.sync.dma_start(out=w_planes[32*q:32*q+4, s:s+n, :].bitcast(I32), in_=stage[4*q:4*q+4, s:s+n, :].bitcast(I32))
+        def load_rows_n(dst, src, lo, hi):
+            nc.sync.dma_start(out=dst[:, lo:hi, :], in_=src[:, lo:hi, :])
+        for gate in ("i","g","f","o"):
+            load_bias2(gate)
+
         load_acts(0)
+        load_stage("i")
+        load_stage("g")
         load_acts(1)
-        for gate in ("i", "g"):
-            load_bias(gate)
-        for gate in ("i", "g"):
-            load_planes(gate, nc.sync, I32)
-            load_words(gate)
+        load_words("i")
+        spread(0, 4)
+        load_words("g")
+        load_stage("f")
+        load_stage("o")
         load_acts(2)
-        load_acts(3)
-        for gate in ("f", "o"):
-            load_bias(gate)
-        load_planes("f", nc.sync, I32)
         load_words("f")
+        spread(4, 4)
         load_words("o")
+        load_acts(3)
+
         for step in range(STEPS):
             if step + 4 < STEPS:
                 load_acts(step + 4)
             load_rows(c_sb, c_rows, step)
 
-        def spread_bias_ig():
+        def spread_bias_units(n, gate):
             bank = psum_back.tile([P, HIDDEN], F32, name="back")
-            for n, gate in enumerate(("i", "g")):
-                for j in range(CHUNKS):
-                    col = 32 * (CHUNKS * n + j)
-                    nc.tensor.matmul(out=bank[:, col:col + 32],
-                                     lhsT=bias_rows[:, GATE_SLOT[gate], P * j:P * (j + 1)],
-                                     rhs=ones[:, 0:32], start=True, stop=True)
+            for j in range(CHUNKS):
+                nc.tensor.matmul(out=bank[:, 32 * j:32 * (j + 1)],
+                                 lhsT=bias_rows[:, GATE_SLOT[gate], P * j:P * (j + 1)],
+                                 rhs=ones[:, 0:32], start=True, stop=True)
             nc.vector.tensor_copy(
-                out=bias_ig[:],
-                in_=bank[:, 0:32 * 2 * CHUNKS].rearrange("p (n w) -> p n w", w=32)[:, :, 0])
+                out=bias_ig[:, CHUNKS * n:CHUNKS * (n + 1)],
+                in_=bank[:, 0:32 * CHUNKS].rearrange("p (n w) -> p n w", w=32)[:, :, 0])
 
         def spread_bias_fo():
             for n, gate in enumerate(("f", "o")):
@@ -154,11 +172,11 @@ def tile_lstmcell_kernel(
                     nc.tensor.transpose(bank[:, u, P * i:P * (i + 1)], row_words[:, u:K // 2:2], identity[:])
             return bank
 
-        def regroup(side, bank):
+        def regroup(side, bank, on_scalar):
             grouped = work.tile([P, 4 * STEP * P], BF16, name="grouped%d" % side, bufs=2, align_bytes=64)
             out = grouped[:].bitcast(F32).rearrange("p (b u) -> p b u", u=2)
             in_ = bank[:].rearrange("p u b -> p b u")
-            if side == 0:
+            if on_scalar:
                 nc.scalar.copy(out=out, in_=in_)
             else:
                 nc.vector.tensor_copy(out=out, in_=in_)
@@ -200,9 +218,9 @@ def tile_lstmcell_kernel(
         def tiles_of(step):
             return range(STEP * step, STEP * (step + 1)) if 0 <= step < STEPS else ()
 
-        def turn_ahead(step):
+        def turn_ahead(step, scalar_sides):
             turned = [transpose_in(step, side) for side in SIDES]
-            return [regroup(side, turned[side]) for side in SIDES]
+            return [regroup(side, turned[side], side in scalar_sides) for side in SIDES]
 
         def quantise_both(step, grouped):
             for side in SIDES:
@@ -213,7 +231,33 @@ def tile_lstmcell_kernel(
             engine.tensor_tensor(out=h_new[:], in0=out_gate_of[t][:], in1=tanh_of[t][:], op=MULT)
             nc.sync.dma_start(out=h_out_rows[:, t, :], in_=h_new[:])
 
-        for step in range(-LEAD_IN, STEPS + 1):
+        def units(gate, n, m):
+            round_, j = m // CHUNKS, m % CHUNKS
+            acc = gate_by_units(gate, round_, j)
+            sig = work.tile([P, ROUND * P], F32, name="sig_" + gate)
+            col = CHUNKS * n + j
+            nc.scalar.activation(out=sig[:], in_=acc[:], func=SIGMOID, bias=bias_ig[:, col:col + 1], scale=1.0)
+            return sig
+
+        def ig_product(m, sig_i, sig_g):
+            ig = work.tile([P, ROUND * P], F32, name="ig", bufs=2 * CHUNKS)
+            nc.gpsimd.tensor_tensor(out=ig[:], in0=sig_i[:], in1=sig_g[:], op=MULT)
+            ig_of[(m // CHUNKS, m % CHUNKS)] = ig
+
+        for step in range(2):
+            grouped = turn_ahead(step, (0,))
+            quantise_both(step, grouped)
+        spread_bias_units(0, "i")
+        sig_i_of = [units("i", 0, m) for m in range(CHUNKS)]
+        spread_bias_units(1, "g")
+        for m in range(CHUNKS):
+            ig_product(m, sig_i_of[m], units("g", 1, m))
+        for step in (2, 3):
+            grouped = turn_ahead(step, ())
+            quantise_both(step, grouped)
+        spread_bias_fo()
+
+        for step in range(STEPS + 1):
             ahead = step + LEAD_IN
             back_of = {}
             for t in tiles_of(step - 1):
@@ -222,8 +266,6 @@ def tile_lstmcell_kernel(
                     cols = slice(P * (t % ROUND), P * (t % ROUND + 1))
                     nc.tensor.transpose(back[:, P * j:P * (j + 1)], ig_of[(t // ROUND, j)][:, cols], identity[:])
                 back_of[t] = back
-            if step == -LEAD_IG:
-                spread_bias_ig()
             for t in tiles_of(step - 1):
                 c_new = work.tile([P, HIDDEN], F32, name="c_new", bufs=6)
                 nc.vector.tensor_tensor(out=c_new[:], in0=back_of[t][:], in1=forget_of[t][:], op=ADD)
@@ -251,25 +293,16 @@ def tile_lstmcell_kernel(
                     else:
                         out_gate_of[t] = sig
             grouped = None
-            if 0 <= step and ahead < STEPS:
-                grouped = turn_ahead(ahead)
+            if ahead < STEPS:
+                grouped = turn_ahead(ahead, (0,))
             sig_of = {}
-            for n, gate in enumerate(("i", "g")):
+            if step + LEAD_IG < STEPS:
                 for m in tiles_of(step + LEAD_IG):
-                    round_, j = m // CHUNKS, m % CHUNKS
-                    acc = gate_by_units(gate, round_, j)
-                    sig = work.tile([P, ROUND * P], F32, name="sig_" + gate)
-                    col = CHUNKS * n + j
-                    nc.scalar.activation(out=sig[:], in_=acc[:], func=SIGMOID, bias=bias_ig[:, col:col + 1], scale=1.0)
-                    sig_of[(gate, m)] = sig
-            for m in tiles_of(step + LEAD_IG):
-                ig = work.tile([P, ROUND * P], F32, name="ig", bufs=2 * CHUNKS)
-                nc.gpsimd.tensor_tensor(out=ig[:], in0=sig_of[("i", m)][:], in1=sig_of[("g", m)][:], op=MULT)
-                ig_of[(m // CHUNKS, m % CHUNKS)] = ig
-            if step == -1:
-                spread_bias_fo()
-            if step < 0:
-                grouped = turn_ahead(ahead)
+                    sig_of[("i", m)] = units("i", 0, m)
+                for m in tiles_of(step + LEAD_IG):
+                    sig_of[("g", m)] = units("g", 1, m)
+                for m in tiles_of(step + LEAD_IG):
+                    ig_product(m, sig_of[("i", m)], sig_of[("g", m)])
             for t in tiles_of(step):
                 forget = work.tile([P, HIDDEN], F32, name="forget")
                 nc.vector.tensor_tensor(out=forget[:], in0=sig_f_of[t][:], in1=c_sb[:, t, :], op=MULT)

@@ -75,7 +75,9 @@ def tile_lstmcell_kernel(
         bias_fo = keep.tile([P, 2, HIDDEN], F32, name="bias_fo")
         bias_ig = keep.tile([P, 2 * CHUNKS], F32, name="bias_ig")
 
+        idle_rows = keep.tile([P, HIDDEN], BF16, name="idle_rows")
         nc.vector.memset(ones[:], 1.0)
+        nc.vector.memset(idle_rows[:].bitcast(F32), 0.0)
         nc.vector.memset(bias_rows[:].bitcast(F32), 0.0)
         nc.vector.memset(w_planes[:].bitcast(I32), 0)
         warm = keep.tile([P, 1], F32, name="warm")
@@ -146,6 +148,11 @@ def tile_lstmcell_kernel(
             if step + 4 < STEPS:
                 load_acts(step + 4)
             load_rows(c_sb, c_rows, step)
+
+        def keep_clock(count):
+            for k in range(count):
+                spare = psum_mx.tile([P, HIDDEN], F32, name="acc")
+                nc.tensor.matmul(out=spare[:], lhsT=ones[:], rhs=idle_rows[:], start=True, stop=True)
 
         def spread_bias_units(n, gate):
             bank = psum_back.tile([P, HIDDEN], F32, name="back")
@@ -244,9 +251,11 @@ def tile_lstmcell_kernel(
             nc.gpsimd.tensor_tensor(out=ig[:], in0=sig_i[:], in1=sig_g[:], op=MULT)
             ig_of[(m // CHUNKS, m % CHUNKS)] = ig
 
+        keep_clock(5)
         for step in range(2):
             grouped = turn_ahead(step, (0,))
             quantise_both(step, grouped)
+        keep_clock(3)
         spread_bias_units(0, "i")
         sig_i_of = [units("i", 0, m) for m in range(CHUNKS)]
         spread_bias_units(1, "g")

@@ -126,21 +126,23 @@ def tile_lstmcell_kernel(
                 nc.sync.dma_start(out=w_planes[32*q:32*q+4, s:s+n, :].bitcast(I32), in_=stage[4*q:4*q+4, s:s+n, :].bitcast(I32))
         def load_rows_n(dst, src, lo, hi):
             nc.sync.dma_start(out=dst[:, lo:hi, :], in_=src[:, lo:hi, :])
-        for gate in ("i","g","f","o"):
+        for gate in ("i", "g"):
             load_bias2(gate)
 
-        load_acts(0)
         load_stage("i")
         load_stage("g")
+        load_acts(0)
         load_acts(1)
-        load_words("i")
         spread(0, 4)
+        load_words("i")
         load_words("g")
         load_stage("f")
         load_stage("o")
         load_acts(2)
         load_words("f")
         spread(4, 4)
+        load_bias("f")
+        load_bias("o")
         load_words("o")
         load_acts(3)
 
@@ -261,10 +263,11 @@ def tile_lstmcell_kernel(
         spread_bias_units(1, "g")
         for m in range(CHUNKS):
             ig_product(m, sig_i_of[m], units("g", 1, m))
-        for step in (2, 3):
-            grouped = turn_ahead(step, ())
-            quantise_both(step, grouped)
+        grouped = turn_ahead(2, (0, 1))
+        quantise_both(2, grouped)
         spread_bias_fo()
+        grouped = turn_ahead(3, (0, 1))
+        quantise_both(3, grouped)
 
         for step in range(STEPS + 1):
             ahead = step + LEAD_IN

@@ -126,26 +126,24 @@ def tile_lstmcell_kernel(
                 nc.sync.dma_start(out=w_planes[32*q:32*q+4, s:s+n, :].bitcast(I32), in_=stage[4*q:4*q+4, s:s+n, :].bitcast(I32))
         def load_rows_n(dst, src, lo, hi):
             nc.sync.dma_start(out=dst[:, lo:hi, :], in_=src[:, lo:hi, :])
-        for gate in ("i", "g"):
+        for gate in ("i", "g", "f"):
             load_bias2(gate)
 
         load_stage("i")
         load_stage("g")
         load_acts(0)
         load_acts(1)
-        spread(0, 4)
+        spread(0,4)
         load_words("i")
         load_words("g")
+        load_acts(2)
         load_stage("f")
         load_stage("o")
-        load_acts(2)
-        load_words("f")
-        spread(4, 4)
-        load_bias("f")
-        load_bias("o")
-        load_words("o")
         load_acts(3)
-
+        load_bias("o")
+        spread(4,4)
+        load_words("f")
+        load_words("o")
         for step in range(STEPS):
             if step + 4 < STEPS:
                 load_acts(step + 4)

@@ -65,10 +65,10 @@ def tile_lstmcell_kernel(
         c_sb = keep.tile([P, TILES, HIDDEN], BF16, name="c_sb")
         act_sb = (x_sb, h_sb)
         act_rows = (x_rows, h_rows)
-        w_codes = keep.tile([P, 8, HIDDEN], U32, name="w_codes", align_bytes=64)
-        w_planes = keep.tile([P, 8, HIDDEN], U8, name="w_planes", align_bytes=64)
-        a_codes = keep.tile([P, 2, BATCH], U32, name="a_codes", align_bytes=64)
-        a_planes = keep.tile([P, 2, BATCH], U8, name="a_planes", align_bytes=64)
+        w_codes = keep.tile([P, 8, HIDDEN], U32, name="w_codes", align_bytes=256)
+        w_planes = keep.tile([P, 8, HIDDEN], U8, name="w_planes", align_bytes=256)
+        a_codes = keep.tile([P, 2, BATCH], U32, name="a_codes", align_bytes=256)
+        a_planes = keep.tile([P, 2, BATCH], U8, name="a_planes", align_bytes=256)
         identity = keep.tile([P, P], F32, name="identity")
         ones = keep.tile([P, P], BF16, name="ones")
         bias_rows = keep.tile([P, 4, HIDDEN], BF16, name="bias_rows")

@@ -255,6 +255,8 @@ def tile_lstmcell_kernel(
         for step in range(2):
             grouped = turn_ahead(step, (0,))
             quantise_both(step, grouped)
+            if step == 0:
+                keep_clock(2)
         keep_clock(3)
         spread_bias_units(0, "i")
         sig_i_of = [units("i", 0, m) for m in range(CHUNKS)]

@@ -286,7 +286,7 @@ def tile_lstmcell_kernel(
                 nc.scalar.activation(out=tanh_c[:], in_=c_new[:], func=TANH)
                 tanh_of[t] = tanh_c
             on_vector = [t for t in tiles_of(step - 1)
-                         if ((t % ROUND == 0 or t % (2 * ROUND) == 2) and t != TILES - ROUND) or step == STEPS]
+                         if (t % 2 == 0 and t <= TILES // 2) or step == STEPS]
             if step == STEPS:
                 on_vector.insert(0, TILES - ROUND)
             for t in tiles_of(step - 1):

from contextlib import ExitStack

import concourse.mybir as mybir
from concourse.masks import make_identity

F32 = mybir.dt.float32
BF16 = mybir.dt.bfloat16
I32 = mybir.dt.int32
U32 = mybir.dt.uint32
U8 = mybir.dt.uint8
FP8X4 = mybir.dt.float8_e4m3fn_x4
SIGMOID = mybir.ActivationFunctionType.Sigmoid
TANH = mybir.ActivationFunctionType.Tanh
ADD = mybir.AluOpType.add
MULT = mybir.AluOpType.mult

P = 128
BATCH = 2048
K = 512
HIDDEN = 512
FLOPS = 2 * BATCH * (2 * K) * (4 * HIDDEN)

TILES = BATCH // P
CHUNKS = HIDDEN // P
ROUND = 4
STEP = 2
STEPS = TILES // STEP
LEAD_IN = 4
LEAD_IG = 2
GATE_SLOT = {"i": 0, "g": 1, "f": 2, "o": 3}
SIDES = (0, 1)


def tile_lstmcell_kernel(
    tc, x, h, c,
    w_ii_words, w_ii_scales, w_hi_words, w_hi_scales, b_ii, b_hi,
    w_if_words, w_if_scales, w_hf_words, w_hf_scales, b_if, b_hf,
    w_ig_words, w_ig_scales, w_hg_words, w_hg_scales, b_ig, b_hg,
    w_io_words, w_io_scales, w_ho_words, w_ho_scales, b_io, b_ho,
    h_out, c_out,
):
    nc = tc.nc
    words_of = {"i": (w_ii_words, w_hi_words), "f": (w_if_words, w_hf_words),
                "g": (w_ig_words, w_hg_words), "o": (w_io_words, w_ho_words)}
    scales_of = {"i": (w_ii_scales, w_hi_scales), "f": (w_if_scales, w_hf_scales),
                 "g": (w_ig_scales, w_hg_scales), "o": (w_io_scales, w_ho_scales)}
    bias_of = {"i": (b_ii, b_hi), "f": (b_if, b_hf), "g": (b_ig, b_hg), "o": (b_io, b_ho)}

    x_rows = x.rearrange("(p t) k -> p t k", t=TILES)
    h_rows = h.rearrange("(p t) k -> p t k", t=TILES)
    c_rows = c.rearrange("(p t) n -> p t n", t=TILES)
    h_out_rows = h_out.rearrange("(p t) n -> p t n", t=TILES)
    c_out_rows = c_out.rearrange("(p t) n -> p t n", t=TILES)

    with ExitStack() as ctx:
        keep = ctx.enter_context(tc.tile_pool(name="keep", bufs=1))
        work = ctx.enter_context(tc.tile_pool(name="work", bufs=4))
        psum_mx = ctx.enter_context(tc.psum_pool(name="psum_mx", bufs=4))
        psum_in = ctx.enter_context(tc.psum_pool(name="psum_in", bufs=2))
        psum_back = ctx.enter_context(tc.psum_pool(name="psum_back", bufs=2))
        ctx.enter_context(tc.manual_schedule())

        x_sb = keep.tile([P, TILES, K], BF16, name="x_sb")
        h_sb = keep.tile([P, TILES, K], BF16, name="h_sb")
        c_sb = keep.tile([P, TILES, HIDDEN], BF16, name="c_sb")
        act_sb = (x_sb, h_sb)
        act_rows = (x_rows, h_rows)
        w_codes = keep.tile([P, 8, HIDDEN], U32, name="w_codes", align_bytes=256)
        w_planes = keep.tile([P, 8, HIDDEN], U8, name="w_planes", align_bytes=256)
        a_codes = keep.tile([P, 2, BATCH], U32, name="a_codes", align_bytes=256)
        a_planes = keep.tile([P, 2, BATCH], U8, name="a_planes", align_bytes=256)
        identity = keep.tile([P, P], F32, name="identity")
        ones = keep.tile([P, P], BF16, name="ones")
        bias_rows = keep.tile([P, 4, HIDDEN], BF16, name="bias_rows")
        bias_fo = keep.tile([P, 2, HIDDEN], F32, name="bias_fo")
        bias_ig = keep.tile([P, 2 * CHUNKS], F32, name="bias_ig")

        idle_rows = keep.tile([P, HIDDEN], BF16, name="idle_rows")
        nc.vector.memset(ones[:], 1.0)
        nc.vector.memset(idle_rows[:].bitcast(F32), 0.0)
        nc.vector.memset(bias_rows[:].bitcast(F32), 0.0)
        nc.vector.memset(w_planes[:].bitcast(I32), 0)
        warm = keep.tile([P, 1], F32, name="warm")
        nc.scalar.activation(out=warm[:], in_=ones[:, 0:1], func=SIGMOID)
        make_identity(nc, identity[:])

        def load_bias(gate):
            for side in SIDES:
                nc.sync.dma_start(out=bias_rows[side:side + 1, GATE_SLOT[gate], :],
                                  in_=bias_of[gate][side].rearrange("(o n) -> o n", o=1))

        def load_rows(dst, src, step):
            cut = slice(STEP * step, STEP * (step + 1))
            nc.sync.dma_start(out=dst[:, cut, :], in_=src[:, cut, :])

        def load_words(gate):
            for side in SIDES:
                slot = 2 * GATE_SLOT[gate] + side
                nc.sync.dma_start(out=w_codes[:, slot, :].bitcast(I32),
                                  in_=words_of[gate][side][0].rearrange("p n t -> p (n t)").bitcast(I32))

        def load_planes(gate, queue, view):
            for side in SIDES:
                slot = 2 * GATE_SLOT[gate] + side
                for quadrant in range(4):
                    queue.dma_start(
                        out=w_planes[32 * quadrant:32 * quadrant + 4, slot, :].bitcast(view),
                        in_=scales_of[gate][side][0, 4 * quadrant:4 * quadrant + 4, :].bitcast(view))

        def load_acts(step):
            for side in SIDES:
                load_rows(act_sb[side], act_rows[side], step)


        stage = keep.tile([16, 8, HIDDEN], U8, name="stage")
        def load_bias2(gate):
            for side in SIDES:
                nc.gpsimd.dma_start(out=bias_rows[side:side + 1, GATE_SLOT[gate], :],
                                  in_=bias_of[gate][side].rearrange("(o n) -> o n", o=1))
        def load_stage(gate):
            for side in SIDES:
                slot = 2 * GATE_SLOT[gate] + side
                nc.sync.dma_start(out=stage[:, slot, :].bitcast(I32), in_=scales_of[gate][side][0].bitcast(I32))
        def spread(s, n):
            for q in range(4):
                nc.sync.dma_start(out=w_planes[32*q:32*q+4, s:s+n, :].bitcast(I32), in_=stage[4*q:4*q+4, s:s+n, :].bitcast(I32))
        def load_rows_n(dst, src, lo, hi):
            nc.sync.dma_start(out=dst[:, lo:hi, :], in_=src[:, lo:hi, :])
        for gate in ("i", "g", "f"):
            load_bias2(gate)

        load_stage("i")
        load_stage("g")
        load_acts(0)
        load_acts(1)
        spread(0,4)
        load_words("i")
        load_words("g")
        load_acts(2)
        load_stage("f")
        load_stage("o")
        load_acts(3)
        load_bias("o")
        spread(4,4)
        load_words("f")
        load_words("o")
        for step in range(STEPS):
            if step + 4 < STEPS:
                load_acts(step + 4)
            load_rows(c_sb, c_rows, step)

        def keep_clock(count):
            for k in range(count):
                spare = psum_mx.tile([P, HIDDEN], F32, name="acc")
                nc.tensor.matmul(out=spare[:], lhsT=ones[:], rhs=idle_rows[:], start=True, stop=True)

        def spread_bias_units(n, gate):
            bank = psum_back.tile([P, HIDDEN], F32, name="back")
            for j in range(CHUNKS):
                nc.tensor.matmul(out=bank[:, 32 * j:32 * (j + 1)],
                                 lhsT=bias_rows[:, GATE_SLOT[gate], P * j:P * (j + 1)],
                                 rhs=ones[:, 0:32], start=True, stop=True)
            nc.vector.tensor_copy(
                out=bias_ig[:, CHUNKS * n:CHUNKS * (n + 1)],
                in_=bank[:, 0:32 * CHUNKS].rearrange("p (n w) -> p n w", w=32)[:, :, 0])

        def spread_bias_fo():
            for n, gate in enumerate(("f", "o")):
                bank = psum_back.tile([P, HIDDEN], F32, name="back")
                nc.tensor.matmul(out=bank[:], lhsT=ones[:], rhs=bias_rows[:, GATE_SLOT[gate], :],
                                 start=True, stop=True)
                nc.vector.tensor_copy(out=bias_fo[:, n, :], in_=bank[:])

        def transpose_in(step, side):
            bank = psum_in.tile([P, 2, STEP * P], F32, name="turned")
            for i in range(STEP):
                row_words = act_sb[side][:, STEP * step + i, :].bitcast(F32)
                for u in range(2):
                    nc.tensor.transpose(bank[:, u, P * i:P * (i + 1)], row_words[:, u:K // 2:2], identity[:])
            return bank

        def regroup(side, bank, on_scalar):
            grouped = work.tile([P, 4 * STEP * P], BF16, name="grouped%d" % side, bufs=2, align_bytes=64)
            out = grouped[:].bitcast(F32).rearrange("p (b u) -> p b u", u=2)
            in_ = bank[:].rearrange("p u b -> p b u")
            if on_scalar:
                nc.scalar.copy(out=out, in_=in_)
            else:
                nc.vector.tensor_copy(out=out, in_=in_)
            return grouped

        def quantise(step, side, grouped):
            cols = slice(STEP * P * step, STEP * P * (step + 1))
            nc.vector.quantize_mx(out=a_codes[:, side, cols].bitcast(FP8X4),
                                  scales=a_planes[:, side, cols], in_=grouped[:])

        def gate_by_rows(gate, t):
            acc = psum_mx.tile([P, HIDDEN], F32, name="acc")
            rows = slice(P * t, P * (t + 1))
            for side in SIDES:
                slot = 2 * GATE_SLOT[gate] + side
                nc.tensor.matmul_mx(out=acc[:],
                                    lhsT=a_codes[:, side, rows].bitcast(FP8X4), lhsT_scale=a_planes[:, side, rows],
                                    rhs=w_codes[:, slot, :].bitcast(FP8X4), rhs_scale=w_planes[:, slot, :],
                                    start=(side == 0), stop=(side == 1))
            return acc

        def gate_by_units(gate, round_, j):
            acc = psum_mx.tile([P, ROUND * P], F32, name="acc")
            units = slice(P * j, P * (j + 1))
            rows = slice(ROUND * P * round_, ROUND * P * (round_ + 1))
            for side in SIDES:
                slot = 2 * GATE_SLOT[gate] + side
                nc.tensor.matmul_mx(out=acc[:],
                                    lhsT=w_codes[:, slot, units].bitcast(FP8X4), lhsT_scale=w_planes[:, slot, units],
                                    rhs=a_codes[:, side, rows].bitcast(FP8X4), rhs_scale=a_planes[:, side, rows],
                                    start=(side == 0), stop=(side == 1))
            return acc

        ig_of = {}
        forget_of = {}
        out_gate_of = {}
        tanh_of = {}

        def tiles_of(step):
            return range(STEP * step, STEP * (step + 1)) if 0 <= step < STEPS else ()

        def turn_ahead(step, scalar_sides):
            turned = [transpose_in(step, side) for side in SIDES]
            return [regroup(side, turned[side], side in scalar_sides) for side in SIDES]

        def quantise_both(step, grouped):
            for side in SIDES:
                quantise(step, side, grouped[side])

        def h_prime(engine, t):
            h_new = work.tile([P, HIDDEN], F32, name="h_new", bufs=6)
            engine.tensor_tensor(out=h_new[:], in0=out_gate_of[t][:], in1=tanh_of[t][:], op=MULT)
            nc.sync.dma_start(out=h_out_rows[:, t, :], in_=h_new[:])

        def units(gate, n, m):
            round_, j = m // CHUNKS, m % CHUNKS
            acc = gate_by_units(gate, round_, j)
            sig = work.tile([P, ROUND * P], F32, name="sig_" + gate)
            col = CHUNKS * n + j
            nc.scalar.activation(out=sig[:], in_=acc[:], func=SIGMOID, bias=bias_ig[:, col:col + 1], scale=1.0)
            return sig

        def ig_product(m, sig_i, sig_g):
            ig = work.tile([P, ROUND * P], F32, name="ig", bufs=2 * CHUNKS)
            nc.gpsimd.tensor_tensor(out=ig[:], in0=sig_i[:], in1=sig_g[:], op=MULT)
            ig_of[(m // CHUNKS, m % CHUNKS)] = ig

        keep_clock(5)
        for step in range(2):
            grouped = turn_ahead(step, (0,))
            quantise_both(step, grouped)
            if step == 0:
                keep_clock(2)
        keep_clock(3)
        spread_bias_units(0, "i")
        sig_i_of = [units("i", 0, m) for m in range(CHUNKS)]
        spread_bias_units(1, "g")
        for m in range(CHUNKS):
            ig_product(m, sig_i_of[m], units("g", 1, m))
        grouped = turn_ahead(2, (0, 1))
        quantise_both(2, grouped)
        spread_bias_fo()
        grouped = turn_ahead(3, (0, 1))
        quantise_both(3, grouped)

        for step in range(STEPS + 1):
            ahead = step + LEAD_IN
            back_of = {}
            for t in tiles_of(step - 1):
                back = psum_back.tile([P, HIDDEN], F32, name="back")
                for j in range(CHUNKS):
                    cols = slice(P * (t % ROUND), P * (t % ROUND + 1))
                    nc.tensor.transpose(back[:, P * j:P * (j + 1)], ig_of[(t // ROUND, j)][:, cols], identity[:])
                back_of[t] = back
            for t in tiles_of(step - 1):
                c_new = work.tile([P, HIDDEN], F32, name="c_new", bufs=6)
                nc.vector.tensor_tensor(out=c_new[:], in0=back_of[t][:], in1=forget_of[t][:], op=ADD)
                nc.sync.dma_start(out=c_out_rows[:, t, :], in_=c_new[:])
                tanh_c = work.tile([P, HIDDEN], F32, name="tanh_c")
                nc.scalar.activation(out=tanh_c[:], in_=c_new[:], func=TANH)
                tanh_of[t] = tanh_c
            on_vector = [t for t in tiles_of(step - 1)
                         if (t % 2 == 0 and t <= TILES // 2) or step == STEPS]
            if step == STEPS:
                on_vector.insert(0, TILES - ROUND)
            for t in tiles_of(step - 1):
                if t not in on_vector and t != TILES - ROUND:
                    h_prime(nc.gpsimd, t)
            sig_f_of = {}
            for n, gate in enumerate(("f", "o")):
                for t in tiles_of(step):
                    acc = gate_by_rows(gate, t)
                    pre = work.tile([P, HIDDEN], F32, name="pre")
                    nc.vector.tensor_tensor(out=pre[:], in0=acc[:], in1=bias_fo[:, n, :], op=ADD)
                    sig = work.tile([P, HIDDEN], F32, name="sig_" + gate, bufs=6)
                    nc.scalar.activation(out=sig[:], in_=pre[:], func=SIGMOID)
                    if gate == "f":
                        sig_f_of[t] = sig
                    else:
                        out_gate_of[t] = sig
            grouped = None
            if ahead < STEPS:
                grouped = turn_ahead(ahead, (0,))
            sig_of = {}
            if step + LEAD_IG < STEPS:
                for m in tiles_of(step + LEAD_IG):
                    sig_of[("i", m)] = units("i", 0, m)
                for m in tiles_of(step + LEAD_IG):
                    sig_of[("g", m)] = units("g", 1, m)
                for m in tiles_of(step + LEAD_IG):
                    ig_product(m, sig_of[("i", m)], sig_of[("g", m)])
            for t in tiles_of(step):
                forget = work.tile([P, HIDDEN], F32, name="forget")
                nc.vector.tensor_tensor(out=forget[:], in0=sig_f_of[t][:], in1=c_sb[:, t, :], op=MULT)
                forget_of[t] = forget
            if grouped:
                quantise_both(ahead, grouped)
            for t in on_vector:
                h_prime(nc.vector, t)
